import numpy as np
import ml_dtypes


def mxq(x, axis, fmt="e4m3"):
    dtype, down = {"e4m3": (ml_dtypes.float8_e4m3fn, 7), "e5m2": (ml_dtypes.float8_e5m2, 14)}[fmt]
    v = np.moveaxis(np.asarray(x, np.float32).astype(ml_dtypes.bfloat16).astype(np.float64), axis, -1)
    blocks = v.reshape(v.shape[:-1] + (-1, 32))
    amax = np.abs(blocks).max(-1, keepdims=True)
    byte = np.maximum(np.where(amax > 0, np.frexp(amax)[1] - 1 + 127, 0) - down, 1)
    scale = np.exp2(byte - 127.0)
    codes = (blocks / scale).astype(np.float32).astype(dtype).astype(np.float64)
    return np.moveaxis((codes * scale).reshape(v.shape), -1, axis)


WIDE = False


def mx_kscale(k):
    if not WIDE:
        return np.ones(k)
    levels = np.array([10, -10, 5, -5, 0])
    a = np.random.permutation(np.resize(levels, k // 512 * 4)).reshape(k // 512, 4)
    idx = np.arange(k)
    return np.exp2(a[idx // 512, idx % 128 // 32])


BF16 = ml_dtypes.bfloat16


def bf(x):
    return np.asarray(x, np.float32).astype(BF16)


def f64(x):
    return np.asarray(x).astype(np.float64)


N, ND, NP, KW = 32, 512, 4, 3
JW = KW - 1
KX = JW * ND


def windows(x):
    return np.moveaxis(x.reshape(N, ND, NP, JW), 1, -1).reshape(N, NP, KX)


def taps(W):
    return W.transpose(2, 1, 0).reshape(KW * ND, ND)


def setup_inputs():
    s, t, u = mx_kscale(KX), mx_kscale(ND), mx_kscale(ND)
    r2 = np.concatenate([s, t]).reshape(KW, ND).T
    r3 = np.concatenate([s, u]).reshape(KW, ND).T
    c = 1.0 / np.sqrt(KW * ND)
    return {'x': bf(np.random.standard_normal((N, ND, JW * NP)) * np.tile(s.reshape(JW, ND).T, (1, NP))),
            'd_h1': bf(np.maximum(np.random.standard_normal((N, ND, NP)), 0.0) * t[:, None]),
            'd1': bf(np.random.standard_normal((N, ND, NP))),
            'W2': bf(np.random.standard_normal((ND, ND, KW)) * c * u[:, None, None] / r2[None]),
            'b2': bf(np.random.standard_normal(ND) * 0.3 * u),
            'W3': bf(np.random.standard_normal((ND, ND, KW)) * c / r3[None]),
            'b3': bf(np.random.standard_normal(ND) * 0.3)}


def reference(x, d_h1, d1, W2, b2, W3, b3):
    xq = mxq(windows(f64(x)), 2, 'e4m3')
    w2, w3 = taps(f64(W2)), taps(f64(W3))
    a2 = (xq @ mxq(w2[:KX], 0, 'e4m3')) + (mxq(f64(d_h1).transpose(0, 2, 1), 2, 'e4m3') @ mxq(w2[KX:], 0, 'e4m3')) + f64(b2)
    h2 = np.maximum(a2, 0.0)
    a3 = (xq @ mxq(w3[:KX], 0, 'e4m3')) + (mxq(h2, 2, 'e4m3') @ mxq(w3[KX:], 0, 'e4m3')) + f64(b3)
    return np.maximum(a3.transpose(0, 2, 1) + f64(d1), 0.0)

@@ -1,0 +1,186 @@
+from contextlib import ExitStack
+
+import concourse.mybir as mybir
+from concourse.masks import make_identity
+
+BF16 = mybir.dt.bfloat16
+F32 = mybir.dt.float32
+U32 = mybir.dt.uint32
+U8 = mybir.dt.uint8
+FP8X4 = mybir.dt.float8_e4m3fn_x4
+RELU = mybir.ActivationFunctionType.Relu
+ADD = mybir.AluOpType.add
+
+P = 128
+PACK = 4
+EVENTS = 32
+SLOTS = 4
+JETS = 2
+PLACES = 3
+CHANNELS = P * PACK
+TOKENS = SLOTS * EVENTS
+CHUNKS = CHANNELS // P
+ROWS_PER_TILE = P // PACK
+TILES_PER_CHUNK = P // ROWS_PER_TILE
+
+FLOPS = 2 * 2 * TOKENS * PLACES * CHANNELS * CHANNELS
+
+
+def tile_dijetresnetblock_pa_s_kernel(tc, x, d_h1, d1, W2, b2, W3, b3, out):
+    nc = tc.nc
+    with ExitStack() as ctx:
+        ctx.enter_context(tc.manual_schedule())
+        keep = ctx.enter_context(tc.tile_pool(name="keep", bufs=1))
+        rows_pool = ctx.enter_context(tc.tile_pool(name="rows", bufs=2 * CHUNKS))
+        stage = ctx.enter_context(tc.tile_pool(name="stage", bufs=4))
+        flipped = ctx.enter_context(tc.psum_pool(name="flipped", bufs=6))
+        sums = ctx.enter_context(tc.psum_pool(name="sums", bufs=1))
+
+        x_rows = keep.tile([P, P, SLOTS * JETS], BF16)
+        nc.sync.dma_start(out=x_rows[:], in_=x.rearrange("b (q r) j -> (b q) r j", q=PACK))
+        dh_rows = keep.tile([P, P, SLOTS], BF16)
+        nc.sync.dma_start(out=dh_rows[:], in_=d_h1.rearrange("b (q r) s -> (b q) r s", q=PACK))
+
+        bias_rows = keep.tile([P, P], BF16)
+        nc.vector.memset(bias_rows[:], 0.0)
+        nc.scalar.dma_start(out=bias_rows[0:CHUNKS, :], in_=b2.rearrange("(c r) -> c r", c=CHUNKS))
+        nc.scalar.dma_start(
+            out=bias_rows[CHUNKS : 2 * CHUNKS, :], in_=b3.rearrange("(c r) -> c r", c=CHUNKS)
+        )
+
+        def load_weight(w):
+            view = w.rearrange("(a o) (q r) k -> (o q) a (r k)", o=ROWS_PER_TILE, q=PACK)
+            chunks = []
+            for c in range(CHUNKS):
+                w_rows = rows_pool.tile([P, TILES_PER_CHUNK, P * PLACES], BF16, tag="w_rows")
+                tiles = slice(c * TILES_PER_CHUNK, (c + 1) * TILES_PER_CHUNK)
+                nc.sync.dma_start(out=w_rows[:], in_=view[:, tiles, :])
+                chunks.append(w_rows)
+            return chunks
+
+        w2_rows = load_weight(W2)
+        d1_rows = keep.tile([P, P, SLOTS], BF16)
+        nc.sync.dma_start(out=d1_rows[:], in_=d1.rearrange("b (c r) s -> (b c) r s", c=CHUNKS))
+        w3_rows = load_weight(W3)
+
+        ident_bf = keep.tile([P, P], BF16)
+        make_identity(nc, ident_bf[:])
+        ident_f32 = keep.tile([P, P], F32)
+        make_identity(nc, ident_f32[:])
+
+        act_codes = keep.tile([P, PLACES, TOKENS], U32, align_bytes=64)
+        act_scales = keep.tile([P, PLACES, TOKENS], U8, align_bytes=64)
+
+        x_t = flipped.tile([P, SLOTS * JETS, P], BF16, tag="flipped")
+        for j in range(SLOTS * JETS):
+            nc.tensor.transpose(out=x_t[:, j, :], in_=x_rows[:, :, j], identity=ident_bf[:])
+        x_grouped = keep.tile([P, JETS, SLOTS, P], BF16, align_bytes=64)
+        nc.scalar.copy(out=x_grouped[:], in_=x_t[:].rearrange("p (s k) f -> p k s f", k=JETS))
+
+        dh_t = flipped.tile([P, SLOTS, P], BF16, tag="flipped")
+        for s in range(SLOTS):
+            nc.tensor.transpose(out=dh_t[:, s, :], in_=dh_rows[:, :, s], identity=ident_bf[:])
+        dh_grouped = keep.tile([P, SLOTS, P], BF16, align_bytes=64)
+        nc.scalar.copy(out=dh_grouped[:], in_=dh_t[:])
+
+        nc.vector.quantize_mx(
+            out=act_codes[:, 0:JETS, :].rearrange("p k t -> p (k t)").bitcast(FP8X4),
+            scales=act_scales[:, 0:JETS, :].rearrange("p k t -> p (k t)"),
+            in_=x_grouped[:].rearrange("p k s f -> p (k s f)"),
+        )
+        nc.vector.quantize_mx(
+            out=act_codes[:, JETS, :].bitcast(FP8X4),
+            scales=act_scales[:, JETS, :],
+            in_=dh_grouped[:].rearrange("p s f -> p (s f)"),
+        )
+
+        bias_t = flipped.tile([P, P], BF16, tag="flipped")
+        nc.tensor.transpose(out=bias_t[:], in_=bias_rows[:], identity=ident_bf[:])
+        bias = keep.tile([P, 2 * CHUNKS], F32)
+        nc.vector.tensor_copy(out=bias[:], in_=bias_t[:, 0 : 2 * CHUNKS])
+
+        def new_weight_operand(name):
+            codes = keep.tile([P, PLACES, CHANNELS], U32, name=name + "_codes", align_bytes=64)
+            scales = keep.tile([P, PLACES, CHANNELS], U8, name=name + "_scales", align_bytes=64)
+            return codes, scales
+
+        def quantise_chunk(w_rows, c, codes, scales):
+            by_place = w_rows[:].rearrange("p a (r k) -> p a k r", k=PLACES)
+            cols = slice(c * P, (c + 1) * P)
+            for k in range(PLACES):
+                w_t = flipped.tile([P, TILES_PER_CHUNK, P], BF16, tag="flipped")
+                for a in range(TILES_PER_CHUNK):
+                    nc.tensor.transpose(
+                        out=w_t[:, a, :], in_=by_place[:, a, k, :], identity=ident_bf[:]
+                    )
+                w_grouped = stage.tile([P, P * PACK], BF16, align_bytes=64)
+                nc.scalar.copy(out=w_grouped[:], in_=w_t[:].rearrange("p a f -> p (a f)"))
+                nc.vector.quantize_mx(
+                    out=codes[:, k, cols].bitcast(FP8X4), scales=scales[:, k, cols], in_=w_grouped[:]
+                )
+
+        def convolve(acc, w_codes, w_scales, dijet_codes, dijet_scales):
+            for c in range(CHUNKS):
+                cols = slice(c * P, (c + 1) * P)
+                for k in range(PLACES):
+                    jet = k < JETS
+                    nc.tensor.matmul_mx(
+                        out=acc[:, c, :],
+                        lhsT=w_codes[:, k, cols].bitcast(FP8X4),
+                        lhsT_scale=w_scales[:, k, cols],
+                        rhs=(act_codes[:, k, :] if jet else dijet_codes).bitcast(FP8X4),
+                        rhs_scale=act_scales[:, k, :] if jet else dijet_scales,
+                        start=(k == 0),
+                        stop=(k == PLACES - 1),
+                    )
+
+        w2_codes, w2_scales = new_weight_operand("w2")
+        w3_codes, w3_scales = new_weight_operand("w3")
+        for c in range(CHUNKS):
+            quantise_chunk(w2_rows[c], c, w2_codes, w2_scales)
+
+        d1_t = flipped.tile([P, SLOTS, P], BF16, tag="flipped")
+        for s in range(SLOTS):
+            nc.tensor.transpose(out=d1_t[:, s, :], in_=d1_rows[:, :, s], identity=ident_bf[:])
+        resid = keep.tile([P, TOKENS, CHUNKS], F32)
+        nc.vector.tensor_tensor(
+            out=resid[:],
+            in0=d1_t[:].rearrange("p s (b c) -> p (s b) c", c=CHUNKS),
+            in1=bias[:, CHUNKS : 2 * CHUNKS].unsqueeze(1).to_broadcast([P, TOKENS, CHUNKS]),
+            op=ADD,
+        )
+
+        quantise_chunk(w3_rows[0], 0, w3_codes, w3_scales)
+
+        a2 = sums.tile([P, CHUNKS, TOKENS], F32)
+        convolve(a2, w2_codes, w2_scales, act_codes[:, JETS, :], act_scales[:, JETS, :])
+        h_grouped = keep.tile([P, TOKENS, PACK], BF16, align_bytes=64)
+        for c in range(CHUNKS):
+            nc.scalar.activation(
+                out=h_grouped[:, :, c], in_=a2[:, c, :], func=RELU, bias=bias[:, c : c + 1], scale=1.0
+            )
+        h_codes = keep.tile([P, TOKENS], U32, align_bytes=64)
+        h_scales = keep.tile([P, TOKENS], U8, align_bytes=64)
+        nc.vector.quantize_mx(
+            out=h_codes[:].bitcast(FP8X4),
+            scales=h_scales[:],
+            in_=h_grouped[:].rearrange("p t c -> p (t c)"),
+        )
+
+        for c in range(1, CHUNKS):
+            quantise_chunk(w3_rows[c], c, w3_codes, w3_scales)
+
+        a3 = sums.tile([P, CHUNKS, TOKENS], F32)
+        convolve(a3, w3_codes, w3_scales, h_codes[:], h_scales[:])
+
+        pre = keep.tile([P, TOKENS, CHUNKS], F32)
+        nc.vector.tensor_tensor(
+            out=pre[:], in0=a3[:].rearrange("p c t -> p t c"), in1=resid[:], op=ADD
+        )
+        by_slot = pre[:].rearrange("p (s b) c -> p s (b c)", s=SLOTS)
+        out_t = flipped.tile([P, SLOTS, P], F32, tag="flipped")
+        for s in range(SLOTS):
+            nc.tensor.transpose(out=out_t[:, s, :], in_=by_slot[:, s, :], identity=ident_f32[:])
+        result = keep.tile([P, P, SLOTS], F32)
+        nc.scalar.activation(out=result[:], in_=out_t[:].rearrange("p s r -> p r s"), func=RELU)
+        nc.sync.dma_start(out=out.rearrange("b (c r) s -> (b c) r s", c=CHUNKS), in_=result[:])

@@ -10,6 +10,7 @@ U8 = mybir.dt.uint8
 FP8X4 = mybir.dt.float8_e4m3fn_x4
 RELU = mybir.ActivationFunctionType.Relu
 ADD = mybir.AluOpType.add
+MAX = mybir.AluOpType.max
 
 P = 128
 PACK = 4
@@ -22,6 +23,9 @@ TOKENS = SLOTS * EVENTS
 CHUNKS = CHANNELS // P
 ROWS_PER_TILE = P // PACK
 TILES_PER_CHUNK = P // ROWS_PER_TILE
+
+GRP = 32
+GROUPS = P // GRP
 
 FLOPS = 2 * 2 * TOKENS * PLACES * CHANNELS * CHANNELS
 
@@ -36,10 +40,10 @@ def tile_dijetresnetblock_pa_s_kernel(tc, x, d_h1, d1, W2, b2, W3, b3, out):
         flipped = ctx.enter_context(tc.psum_pool(name="flipped", bufs=6))
         sums = ctx.enter_context(tc.psum_pool(name="sums", bufs=1))
 
-        x_rows = keep.tile([P, P, SLOTS * JETS], BF16)
-        nc.sync.dma_start(out=x_rows[:], in_=x.rearrange("b (q r) j -> (b q) r j", q=PACK))
         dh_rows = keep.tile([P, P, SLOTS], BF16)
         nc.sync.dma_start(out=dh_rows[:], in_=d_h1.rearrange("b (q r) s -> (b q) r s", q=PACK))
+        x_rows = keep.tile([P, P, SLOTS * JETS], BF16)
+        nc.sync.dma_start(out=x_rows[:], in_=x.rearrange("b (q r) j -> (b q) r j", q=PACK))
 
         bias_rows = keep.tile([P, P], BF16)
         nc.vector.memset(bias_rows[:], 0.0)
@@ -59,23 +63,19 @@ def tile_dijetresnetblock_pa_s_kernel(tc, x, d_h1, d1, W2, b2, W3, b3, out):
             return chunks
 
         w2_rows = load_weight(W2)
-        d1_rows = keep.tile([P, P, SLOTS], BF16)
-        nc.sync.dma_start(out=d1_rows[:], in_=d1.rearrange("b (c r) s -> (b c) r s", c=CHUNKS))
         w3_rows = load_weight(W3)
+        d1_rows = keep.tile([P, CHUNKS, GRP, SLOTS], BF16)
+        d1_view = d1.rearrange("b (c g r) s -> g b c (r s)", c=CHUNKS, g=GROUPS)
+        for g in range(GROUPS):
+            nc.sync.dma_start(
+                out=d1_rows[GRP * g : GRP * g + GRP].rearrange("p c r s -> p c (r s)"), in_=d1_view[g]
+            )
 
         ident_bf = keep.tile([P, P], BF16)
         make_identity(nc, ident_bf[:])
-        ident_f32 = keep.tile([P, P], F32)
-        make_identity(nc, ident_f32[:])
 
         act_codes = keep.tile([P, PLACES, TOKENS], U32, align_bytes=64)
         act_scales = keep.tile([P, PLACES, TOKENS], U8, align_bytes=64)
-
-        x_t = flipped.tile([P, SLOTS * JETS, P], BF16, tag="flipped")
-        for j in range(SLOTS * JETS):
-            nc.tensor.transpose(out=x_t[:, j, :], in_=x_rows[:, :, j], identity=ident_bf[:])
-        x_grouped = keep.tile([P, JETS, SLOTS, P], BF16, align_bytes=64)
-        nc.scalar.copy(out=x_grouped[:], in_=x_t[:].rearrange("p (s k) f -> p k s f", k=JETS))
 
         dh_t = flipped.tile([P, SLOTS, P], BF16, tag="flipped")
         for s in range(SLOTS):
@@ -83,21 +83,22 @@ def tile_dijetresnetblock_pa_s_kernel(tc, x, d_h1, d1, W2, b2, W3, b3, out):
         dh_grouped = keep.tile([P, SLOTS, P], BF16, align_bytes=64)
         nc.scalar.copy(out=dh_grouped[:], in_=dh_t[:])
 
-        nc.vector.quantize_mx(
-            out=act_codes[:, 0:JETS, :].rearrange("p k t -> p (k t)").bitcast(FP8X4),
-            scales=act_scales[:, 0:JETS, :].rearrange("p k t -> p (k t)"),
-            in_=x_grouped[:].rearrange("p k s f -> p (k s f)"),
-        )
+        x_t = flipped.tile([P, SLOTS * JETS, P], BF16, tag="flipped")
+        for j in range(SLOTS * JETS):
+            nc.tensor.transpose(out=x_t[:, j, :], in_=x_rows[:, :, j], identity=ident_bf[:])
+        x_grouped = keep.tile([P, JETS, SLOTS, P], BF16, align_bytes=64)
+        nc.scalar.copy(out=x_grouped[:], in_=x_t[:].rearrange("p (s k) f -> p k s f", k=JETS))
+
         nc.vector.quantize_mx(
             out=act_codes[:, JETS, :].bitcast(FP8X4),
             scales=act_scales[:, JETS, :],
             in_=dh_grouped[:].rearrange("p s f -> p (s f)"),
         )
-
-        bias_t = flipped.tile([P, P], BF16, tag="flipped")
-        nc.tensor.transpose(out=bias_t[:], in_=bias_rows[:], identity=ident_bf[:])
-        bias = keep.tile([P, 2 * CHUNKS], F32)
-        nc.vector.tensor_copy(out=bias[:], in_=bias_t[:, 0 : 2 * CHUNKS])
+        nc.vector.quantize_mx(
+            out=act_codes[:, 0:JETS, :].rearrange("p k t -> p (k t)").bitcast(FP8X4),
+            scales=act_scales[:, 0:JETS, :].rearrange("p k t -> p (k t)"),
+            in_=x_grouped[:].rearrange("p k s f -> p (k s f)"),
+        )
 
         def new_weight_operand(name):
             codes = keep.tile([P, PLACES, CHANNELS], U32, name=name + "_codes", align_bytes=64)
@@ -119,45 +120,48 @@ def tile_dijetresnetblock_pa_s_kernel(tc, x, d_h1, d1, W2, b2, W3, b3, out):
                     out=codes[:, k, cols].bitcast(FP8X4), scales=scales[:, k, cols], in_=w_grouped[:]
                 )
 
-        def convolve(acc, w_codes, w_scales, dijet_codes, dijet_scales):
-            for c in range(CHUNKS):
-                cols = slice(c * P, (c + 1) * P)
-                for k in range(PLACES):
-                    jet = k < JETS
-                    nc.tensor.matmul_mx(
-                        out=acc[:, c, :],
-                        lhsT=w_codes[:, k, cols].bitcast(FP8X4),
-                        lhsT_scale=w_scales[:, k, cols],
-                        rhs=(act_codes[:, k, :] if jet else dijet_codes).bitcast(FP8X4),
-                        rhs_scale=act_scales[:, k, :] if jet else dijet_scales,
-                        start=(k == 0),
-                        stop=(k == PLACES - 1),
-                    )
+        def convolve(acc, c, w_codes, w_scales, dijet_codes, dijet_scales):
+            cols = slice(c * P, (c + 1) * P)
+            for k in range(PLACES):
+                jet = k < JETS
+                nc.tensor.matmul_mx(
+                    out=acc,
+                    lhsT=w_codes[:, k, cols].bitcast(FP8X4),
+                    lhsT_scale=w_scales[:, k, cols],
+                    rhs=(act_codes[:, k, :] if jet else dijet_codes).bitcast(FP8X4),
+                    rhs_scale=act_scales[:, k, :] if jet else dijet_scales,
+                    start=(k == 0),
+                    stop=(k == PLACES - 1),
+                )
 
         w2_codes, w2_scales = new_weight_operand("w2")
         w3_codes, w3_scales = new_weight_operand("w3")
-        for c in range(CHUNKS):
+        quantise_chunk(w2_rows[0], 0, w2_codes, w2_scales)
+        bias_t = flipped.tile([P, P], BF16, tag="flipped")
+        nc.tensor.transpose(out=bias_t[:], in_=bias_rows[:], identity=ident_bf[:])
+        bias = keep.tile([P, 2 * CHUNKS], F32)
+        nc.vector.tensor_copy(out=bias[:], in_=bias_t[:, 0 : 2 * CHUNKS])
+        spread = keep.tile([P, CHUNKS, EVENTS], F32, align_bytes=64)
+        nc.vector.tensor_copy(
+            out=spread[:], in_=bias[:, CHUNKS : 2 * CHUNKS].unsqueeze(2).to_broadcast([P, CHUNKS, EVENTS])
+        )
+        for c in range(1, CHUNKS):
             quantise_chunk(w2_rows[c], c, w2_codes, w2_scales)
 
-        d1_t = flipped.tile([P, SLOTS, P], BF16, tag="flipped")
-        for s in range(SLOTS):
-            nc.tensor.transpose(out=d1_t[:, s, :], in_=d1_rows[:, :, s], identity=ident_bf[:])
-        resid = keep.tile([P, TOKENS, CHUNKS], F32)
-        nc.vector.tensor_tensor(
-            out=resid[:],
-            in0=d1_t[:].rearrange("p s (b c) -> p (s b) c", c=CHUNKS),
-            in1=bias[:, CHUNKS : 2 * CHUNKS].unsqueeze(1).to_broadcast([P, TOKENS, CHUNKS]),
-            op=ADD,
+        b3_rows = keep.tile([P, CHUNKS, GRP], F32, align_bytes=64)
+        nc.vector.transpose(
+            out=b3_rows[:].rearrange("p c r -> p (c r)"), in_=spread[:].rearrange("p c b -> p (c b)")
         )
 
         quantise_chunk(w3_rows[0], 0, w3_codes, w3_scales)
 
         a2 = sums.tile([P, CHUNKS, TOKENS], F32)
-        convolve(a2, w2_codes, w2_scales, act_codes[:, JETS, :], act_scales[:, JETS, :])
+        for c in range(CHUNKS):
+            convolve(a2[:, c, :], c, w2_codes, w2_scales, act_codes[:, JETS, :], act_scales[:, JETS, :])
         h_grouped = keep.tile([P, TOKENS, PACK], BF16, align_bytes=64)
         for c in range(CHUNKS):
-            nc.scalar.activation(
-                out=h_grouped[:, :, c], in_=a2[:, c, :], func=RELU, bias=bias[:, c : c + 1], scale=1.0
+            nc.vector.tensor_scalar(
+                out=h_grouped[:, :, c], in0=a2[:, c, :], scalar1=bias[:, c : c + 1], scalar2=0.0, op0=ADD, op1=MAX
             )
         h_codes = keep.tile([P, TOKENS], U32, align_bytes=64)
         h_scales = keep.tile([P, TOKENS], U8, align_bytes=64)
@@ -167,20 +171,55 @@ def tile_dijetresnetblock_pa_s_kernel(tc, x, d_h1, d1, W2, b2, W3, b3, out):
             in_=h_grouped[:].rearrange("p t c -> p (t c)"),
         )
 
-        for c in range(1, CHUNKS):
+        for c in range(1, CHUNKS - 1):
             quantise_chunk(w3_rows[c], c, w3_codes, w3_scales)
-
-        a3 = sums.tile([P, CHUNKS, TOKENS], F32)
-        convolve(a3, w3_codes, w3_scales, h_codes[:], h_scales[:])
-
-        pre = keep.tile([P, TOKENS, CHUNKS], F32)
+        resid = keep.tile([P, CHUNKS, GRP, SLOTS], F32)
         nc.vector.tensor_tensor(
-            out=pre[:], in0=a3[:].rearrange("p c t -> p t c"), in1=resid[:], op=ADD
+            out=resid[:].rearrange("p c r s -> p (c r) s"),
+            in0=d1_rows[:].rearrange("p c r s -> p (c r) s"),
+            in1=b3_rows[:].rearrange("p c r -> p (c r)").unsqueeze(2).to_broadcast([P, P, SLOTS]),
+            op=ADD,
         )
-        by_slot = pre[:].rearrange("p (s b) c -> p s (b c)", s=SLOTS)
-        out_t = flipped.tile([P, SLOTS, P], F32, tag="flipped")
-        for s in range(SLOTS):
-            nc.tensor.transpose(out=out_t[:, s, :], in_=by_slot[:, s, :], identity=ident_f32[:])
-        result = keep.tile([P, P, SLOTS], F32)
-        nc.scalar.activation(out=result[:], in_=out_t[:].rearrange("p s r -> p r s"), func=RELU)
-        nc.sync.dma_start(out=out.rearrange("b (c r) s -> (b c) r s", c=CHUNKS), in_=result[:])
+        quantise_chunk(w3_rows[CHUNKS - 1], CHUNKS - 1, w3_codes, w3_scales)
+
+        turned = keep.tile([P, CHUNKS, SLOTS, GRP], F32, align_bytes=64)
+        pre = keep.tile([P, CHUNKS, GRP, SLOTS], F32)
+        result = keep.tile([P, CHUNKS, GRP, SLOTS], F32)
+        a3_first = sums.tile([P, CHUNKS - 1, TOKENS], F32)
+        a3_last = flipped.tile([P, TOKENS], F32, tag="flipped")
+
+        def sums_of(c):
+            return a3_first[:, c, :] if c < CHUNKS - 1 else a3_last[:]
+
+        for c in range(CHUNKS):
+            convolve(sums_of(c), c, w3_codes, w3_scales, h_codes[:], h_scales[:])
+
+        def turn(c):
+            nc.vector.transpose(out=turned[:, c].rearrange("p s r -> p (s r)"), in_=sums_of(c))
+
+        def finish(lo, hi, adder):
+            adder.tensor_tensor(
+                out=pre[:, lo:hi],
+                in0=turned[:, lo:hi].rearrange("p c s r -> p c r s"),
+                in1=resid[:, lo:hi],
+                op=ADD,
+            )
+            nc.scalar.activation(out=result[:, lo:hi], in_=pre[:, lo:hi], func=RELU)
+
+        out_view = out.rearrange("b (c g r) s -> g b c (r s)", c=CHUNKS, g=GROUPS)
+
+        def store(lo, hi, queues):
+            for g in range(GROUPS):
+                queues[g % len(queues)].dma_start(
+                    out=out_view[g][:, lo:hi],
+                    in_=result[GRP * g : GRP * g + GRP, lo:hi].rearrange("p c r s -> p c (r s)"),
+                )
+
+        turn(0)
+        turn(1)
+        finish(0, 2, nc.gpsimd)
+        turn(2)
+        turn(3)
+        finish(2, CHUNKS, nc.vector)
+        store(0, 2, [nc.sync])
+        store(2, CHUNKS, [nc.scalar, nc.sync])

from contextlib import ExitStack

import concourse.mybir as mybir
from concourse.masks import make_identity

BF16 = mybir.dt.bfloat16
F32 = mybir.dt.float32
U32 = mybir.dt.uint32
U8 = mybir.dt.uint8
FP8X4 = mybir.dt.float8_e4m3fn_x4
RELU = mybir.ActivationFunctionType.Relu
ADD = mybir.AluOpType.add
MAX = mybir.AluOpType.max

P = 128
PACK = 4
EVENTS = 32
SLOTS = 4
JETS = 2
PLACES = 3
CHANNELS = P * PACK
TOKENS = SLOTS * EVENTS
CHUNKS = CHANNELS // P
ROWS_PER_TILE = P // PACK
TILES_PER_CHUNK = P // ROWS_PER_TILE

GRP = 32
GROUPS = P // GRP

FLOPS = 2 * 2 * TOKENS * PLACES * CHANNELS * CHANNELS


def tile_dijetresnetblock_pa_s_kernel(tc, x, d_h1, d1, W2, b2, W3, b3, out):
    nc = tc.nc
    with ExitStack() as ctx:
        ctx.enter_context(tc.manual_schedule())
        keep = ctx.enter_context(tc.tile_pool(name="keep", bufs=1))
        rows_pool = ctx.enter_context(tc.tile_pool(name="rows", bufs=2 * CHUNKS))
        stage = ctx.enter_context(tc.tile_pool(name="stage", bufs=4))
        flipped = ctx.enter_context(tc.psum_pool(name="flipped", bufs=6))
        sums = ctx.enter_context(tc.psum_pool(name="sums", bufs=1))

        dh_rows = keep.tile([P, P, SLOTS], BF16)
        nc.sync.dma_start(out=dh_rows[:], in_=d_h1.rearrange("b (q r) s -> (b q) r s", q=PACK))
        x_rows = keep.tile([P, P, SLOTS * JETS], BF16)
        nc.sync.dma_start(out=x_rows[:], in_=x.rearrange("b (q r) j -> (b q) r j", q=PACK))

        bias_rows = keep.tile([P, P], BF16)
        nc.vector.memset(bias_rows[:], 0.0)
        nc.scalar.dma_start(out=bias_rows[0:CHUNKS, :], in_=b2.rearrange("(c r) -> c r", c=CHUNKS))
        nc.scalar.dma_start(
            out=bias_rows[CHUNKS : 2 * CHUNKS, :], in_=b3.rearrange("(c r) -> c r", c=CHUNKS)
        )

        def load_weight(w):
            view = w.rearrange("(a o) (q r) k -> (o q) a (r k)", o=ROWS_PER_TILE, q=PACK)
            chunks = []
            for c in range(CHUNKS):
                w_rows = rows_pool.tile([P, TILES_PER_CHUNK, P * PLACES], BF16, tag="w_rows")
                tiles = slice(c * TILES_PER_CHUNK, (c + 1) * TILES_PER_CHUNK)
                nc.sync.dma_start(out=w_rows[:], in_=view[:, tiles, :])
                chunks.append(w_rows)
            return chunks

        w2_rows = load_weight(W2)
        w3_rows = load_weight(W3)
        d1_rows = keep.tile([P, CHUNKS, GRP, SLOTS], BF16)
        d1_view = d1.rearrange("b (c g r) s -> g b c (r s)", c=CHUNKS, g=GROUPS)
        for g in range(GROUPS):
            nc.sync.dma_start(
                out=d1_rows[GRP * g : GRP * g + GRP].rearrange("p c r s -> p c (r s)"), in_=d1_view[g]
            )

        ident_bf = keep.tile([P, P], BF16)
        make_identity(nc, ident_bf[:])

        act_codes = keep.tile([P, PLACES, TOKENS], U32, align_bytes=64)
        act_scales = keep.tile([P, PLACES, TOKENS], U8, align_bytes=64)

        dh_t = flipped.tile([P, SLOTS, P], BF16, tag="flipped")
        for s in range(SLOTS):
            nc.tensor.transpose(out=dh_t[:, s, :], in_=dh_rows[:, :, s], identity=ident_bf[:])
        dh_grouped = keep.tile([P, SLOTS, P], BF16, align_bytes=64)
        nc.scalar.copy(out=dh_grouped[:], in_=dh_t[:])

        x_t = flipped.tile([P, SLOTS * JETS, P], BF16, tag="flipped")
        for j in range(SLOTS * JETS):
            nc.tensor.transpose(out=x_t[:, j, :], in_=x_rows[:, :, j], identity=ident_bf[:])
        x_grouped = keep.tile([P, JETS, SLOTS, P], BF16, align_bytes=64)
        nc.scalar.copy(out=x_grouped[:], in_=x_t[:].rearrange("p (s k) f -> p k s f", k=JETS))

        nc.vector.quantize_mx(
            out=act_codes[:, JETS, :].bitcast(FP8X4),
            scales=act_scales[:, JETS, :],
            in_=dh_grouped[:].rearrange("p s f -> p (s f)"),
        )
        nc.vector.quantize_mx(
            out=act_codes[:, 0:JETS, :].rearrange("p k t -> p (k t)").bitcast(FP8X4),
            scales=act_scales[:, 0:JETS, :].rearrange("p k t -> p (k t)"),
            in_=x_grouped[:].rearrange("p k s f -> p (k s f)"),
        )

        def new_weight_operand(name):
            codes = keep.tile([P, PLACES, CHANNELS], U32, name=name + "_codes", align_bytes=64)
            scales = keep.tile([P, PLACES, CHANNELS], U8, name=name + "_scales", align_bytes=64)
            return codes, scales

        def quantise_chunk(w_rows, c, codes, scales):
            by_place = w_rows[:].rearrange("p a (r k) -> p a k r", k=PLACES)
            cols = slice(c * P, (c + 1) * P)
            for k in range(PLACES):
                w_t = flipped.tile([P, TILES_PER_CHUNK, P], BF16, tag="flipped")
                for a in range(TILES_PER_CHUNK):
                    nc.tensor.transpose(
                        out=w_t[:, a, :], in_=by_place[:, a, k, :], identity=ident_bf[:]
                    )
                w_grouped = stage.tile([P, P * PACK], BF16, align_bytes=64)
                nc.scalar.copy(out=w_grouped[:], in_=w_t[:].rearrange("p a f -> p (a f)"))
                nc.vector.quantize_mx(
                    out=codes[:, k, cols].bitcast(FP8X4), scales=scales[:, k, cols], in_=w_grouped[:]
                )

        def convolve(acc, c, w_codes, w_scales, dijet_codes, dijet_scales):
            cols = slice(c * P, (c + 1) * P)
            for k in range(PLACES):
                jet = k < JETS
                nc.tensor.matmul_mx(
                    out=acc,
                    lhsT=w_codes[:, k, cols].bitcast(FP8X4),
                    lhsT_scale=w_scales[:, k, cols],
                    rhs=(act_codes[:, k, :] if jet else dijet_codes).bitcast(FP8X4),
                    rhs_scale=act_scales[:, k, :] if jet else dijet_scales,
                    start=(k == 0),
                    stop=(k == PLACES - 1),
                )

        w2_codes, w2_scales = new_weight_operand("w2")
        w3_codes, w3_scales = new_weight_operand("w3")
        quantise_chunk(w2_rows[0], 0, w2_codes, w2_scales)
        bias_t = flipped.tile([P, P], BF16, tag="flipped")
        nc.tensor.transpose(out=bias_t[:], in_=bias_rows[:], identity=ident_bf[:])
        bias = keep.tile([P, 2 * CHUNKS], F32)
        nc.vector.tensor_copy(out=bias[:], in_=bias_t[:, 0 : 2 * CHUNKS])
        spread = keep.tile([P, CHUNKS, EVENTS], F32, align_bytes=64)
        nc.vector.tensor_copy(
            out=spread[:], in_=bias[:, CHUNKS : 2 * CHUNKS].unsqueeze(2).to_broadcast([P, CHUNKS, EVENTS])
        )
        for c in range(1, CHUNKS):
            quantise_chunk(w2_rows[c], c, w2_codes, w2_scales)

        b3_rows = keep.tile([P, CHUNKS, GRP], F32, align_bytes=64)
        nc.vector.transpose(
            out=b3_rows[:].rearrange("p c r -> p (c r)"), in_=spread[:].rearrange("p c b -> p (c b)")
        )

        quantise_chunk(w3_rows[0], 0, w3_codes, w3_scales)

        a2 = sums.tile([P, CHUNKS, TOKENS], F32)
        for c in range(CHUNKS):
            convolve(a2[:, c, :], c, w2_codes, w2_scales, act_codes[:, JETS, :], act_scales[:, JETS, :])
        h_grouped = keep.tile([P, TOKENS, PACK], BF16, align_bytes=64)
        for c in range(CHUNKS):
            nc.vector.tensor_scalar(
                out=h_grouped[:, :, c], in0=a2[:, c, :], scalar1=bias[:, c : c + 1], scalar2=0.0, op0=ADD, op1=MAX
            )
        h_codes = keep.tile([P, TOKENS], U32, align_bytes=64)
        h_scales = keep.tile([P, TOKENS], U8, align_bytes=64)
        nc.vector.quantize_mx(
            out=h_codes[:].bitcast(FP8X4),
            scales=h_scales[:],
            in_=h_grouped[:].rearrange("p t c -> p (t c)"),
        )

        for c in range(1, CHUNKS - 1):
            quantise_chunk(w3_rows[c], c, w3_codes, w3_scales)
        resid = keep.tile([P, CHUNKS, GRP, SLOTS], F32)
        nc.vector.tensor_tensor(
            out=resid[:].rearrange("p c r s -> p (c r) s"),
            in0=d1_rows[:].rearrange("p c r s -> p (c r) s"),
            in1=b3_rows[:].rearrange("p c r -> p (c r)").unsqueeze(2).to_broadcast([P, P, SLOTS]),
            op=ADD,
        )
        quantise_chunk(w3_rows[CHUNKS - 1], CHUNKS - 1, w3_codes, w3_scales)

        turned = keep.tile([P, CHUNKS, SLOTS, GRP], F32, align_bytes=64)
        pre = keep.tile([P, CHUNKS, GRP, SLOTS], F32)
        result = keep.tile([P, CHUNKS, GRP, SLOTS], F32)
        a3_first = sums.tile([P, CHUNKS - 1, TOKENS], F32)
        a3_last = flipped.tile([P, TOKENS], F32, tag="flipped")

        def sums_of(c):
            return a3_first[:, c, :] if c < CHUNKS - 1 else a3_last[:]

        for c in range(CHUNKS):
            convolve(sums_of(c), c, w3_codes, w3_scales, h_codes[:], h_scales[:])

        def turn(c):
            nc.vector.transpose(out=turned[:, c].rearrange("p s r -> p (s r)"), in_=sums_of(c))

        def finish(lo, hi, adder):
            adder.tensor_tensor(
                out=pre[:, lo:hi],
                in0=turned[:, lo:hi].rearrange("p c s r -> p c r s"),
                in1=resid[:, lo:hi],
                op=ADD,
            )
            nc.scalar.activation(out=result[:, lo:hi], in_=pre[:, lo:hi], func=RELU)

        out_view = out.rearrange("b (c g r) s -> g b c (r s)", c=CHUNKS, g=GROUPS)

        def store(lo, hi, queues):
            for g in range(GROUPS):
                queues[g % len(queues)].dma_start(
                    out=out_view[g][:, lo:hi],
                    in_=result[GRP * g : GRP * g + GRP, lo:hi].rearrange("p c r s -> p c (r s)"),
                )

        turn(0)
        turn(1)
        finish(0, 2, nc.gpsimd)
        turn(2)
        turn(3)
        finish(2, CHUNKS, nc.vector)
        store(0, 2, [nc.sync])
        store(2, CHUNKS, [nc.scalar, nc.sync])
